import numpy as np
import ml_dtypes


def mxq(x, axis, fmt="e4m3"):
    dtype, down = {"e4m3": (ml_dtypes.float8_e4m3fn, 7), "e5m2": (ml_dtypes.float8_e5m2, 14)}[fmt]
    v = np.moveaxis(np.asarray(x, np.float32).astype(ml_dtypes.bfloat16).astype(np.float64), axis, -1)
    blocks = v.reshape(v.shape[:-1] + (-1, 32))
    amax = np.abs(blocks).max(-1, keepdims=True)
    byte = np.maximum(np.where(amax > 0, np.frexp(amax)[1] - 1 + 127, 0) - down, 1)
    scale = np.exp2(byte - 127.0)
    codes = (blocks / scale).astype(np.float32).astype(dtype).astype(np.float64)
    return np.moveaxis((codes * scale).reshape(v.shape), -1, axis)


WIDE = False


def mx_kscale(k):
    if not WIDE:
        return np.ones(k)
    levels = np.array([10, -10, 5, -5, 0])
    if k % 512:
        return np.exp2(np.random.permutation(np.resize(levels, k // 32))).repeat(32)
    a = np.empty((k // 512, 16))
    for p in range(k // 512):
        a[p, :8] = np.random.permutation(np.resize(levels, 8))
        for g in range(8):
            far = levels[np.abs(levels - a[p, g]) >= 10]
            a[p, g + 8] = far[np.random.randint(len(far))]
    return np.exp2(a.ravel()).repeat(32)


BF16 = ml_dtypes.bfloat16


def bf(x):
    return np.asarray(x, np.float32).astype(BF16)


def f64(x):
    return np.asarray(x).astype(np.float64)


N, NFEAT, NHEADS, NHID, NCLASS = 1024, 512, 4, 128, 128
P = 0.08


def elu(v):
    return np.where(v > 0, v, np.exp(np.minimum(v, 0.0)) - 1.0)


def setup_inputs():
    s, t = mx_kscale(NFEAT), mx_kscale(N)
    edges = np.random.random((N, N)) < P
    return {"x": bf(np.random.standard_normal((N, NFEAT)) * s / t[:, None]),
            "adj": bf(edges * (0.5 + np.random.random((N, N))) * t),
            "W0": bf(np.random.standard_normal((NHEADS, NFEAT, NHID)) * 1.5 / np.sqrt(NFEAT * P * N) / s[:, None])}


def reference(x, adj, W0):
    h = mxq(f64(x), 1, "e4m3") @ mxq(f64(W0), 1, "e4m3")
    hp = mxq(f64(adj), 1, "e4m3") @ mxq(h, 1, "e4m3")
    return elu(hp).transpose(1, 0, 2).reshape(N, NHEADS * NHID)

@@ -1,0 +1,226 @@
+from contextlib import ExitStack
+
+import concourse.mybir as mybir
+from concourse.masks import make_identity
+
+FLOPS = 2 * 1024 * 512 * 512 + 2 * 1024 * 1024 * 512
+
+F32 = mybir.dt.float32
+BF16 = mybir.dt.bfloat16
+U32 = mybir.dt.uint32
+U8 = mybir.dt.uint8
+FP8X4 = mybir.dt.float8_e4m3fn_x4
+ALU = mybir.AluOpType
+ACTF = mybir.ActivationFunctionType
+
+P = 128
+G_BANK_DT = F32
+TP_BANKS = 3
+ACC_BANKS = 5
+
+
+def tile_gat_pa_kernel(tc, x, adj, W0, out):
+    nc = tc.nc
+    with ExitStack() as ctx:
+        sb = ctx.enter_context(tc.tile_pool(name="sb", bufs=1))
+        ps = ctx.enter_context(tc.psum_pool(name="ps", bufs=1))
+        ctx.enter_context(tc.manual_schedule())
+
+        x_raw, x_tp, x_grp, x_cod, x_scl = {}, {}, {}, {}, {}
+        w_raw, w_grp, w_cod, w_scl = {}, {}, {}, {}
+        a_raw, a_tp, a_grp, a_cod, a_scl = {}, {}, {}, {}, {}
+        g_ps, g_grp, g_cod, g_scl = {}, {}, {}, {}
+        p_ps, e_sb, q_sb = {}, {}, {}
+
+        def load_x(g, b):
+            x_raw[g, b] = sb.tile([P, 2, 512], BF16, name="x_raw%d%d" % (g, b))
+            rows = x[512 * g:512 * (g + 1), :].rearrange("(m t) k -> m t k", t=4)
+            nc.sync.dma_start(out=x_raw[g, b][:], in_=rows[:, 2 * b:2 * b + 2, :])
+
+        def load_w(a):
+            w_raw[a] = sb.tile([P, 2, 4, P], BF16, name="w_raw%d" % a)
+            nc.sync.dma_start(out=w_raw[a][:], in_=W0[2 * a:2 * a + 2].rearrange("h (p j) c -> p h j c", j=4))
+
+        def load_adj(i):
+            a_raw[i] = sb.tile([P, 1024], BF16, name="a_raw%d" % i)
+            nc.sync.dma_start(out=a_raw[i][:], in_=adj[P * i:P * (i + 1), :])
+
+        load_x(0, 0)
+        load_x(0, 1)
+        load_x(1, 0)
+        load_w(0)
+        load_x(1, 1)
+        load_w(1)
+        for i in range(8):
+            load_adj(i)
+
+        zeros = sb.tile([P, 512], BF16, name="zeros")
+        nc.vector.memset(zeros[:], 0.0)
+        idle_ps = ps.tile([P, 512], F32, name="idle_ps", tag="acc", bufs=ACC_BANKS)
+        exp_in = sb.tile([P, 1], F32, name="exp_in")
+        exp_out = sb.tile([P, 1], F32, name="exp_out")
+        nc.vector.memset(exp_in[:], 0.0)
+        nc.scalar.activation(out=exp_out[:], in_=exp_in[:], func=ACTF.Exp)
+        ident = sb.tile([P, P], F32, name="ident")
+        make_identity(nc, ident[:])
+
+        def keep_clock(n):
+            for r in range(n):
+                nc.tensor.matmul(out=idle_ps[:], lhsT=zeros[:, 0:P], rhs=zeros[:], start=True, stop=True)
+
+        def transpose_words(name, raw2d):
+            bank = ps.tile([P, 4, P], F32, name=name, tag="tp", bufs=TP_BANKS)
+            words = raw2d.bitcast(F32)
+            for s in range(2):
+                for u in range(2):
+                    nc.tensor.transpose(bank[:, 2 * s + u, :], words[:, 256 * s + u:256 * (s + 1):2], ident[:])
+            return bank
+
+        def group_words(name, bank):
+            grp = sb.tile([P, 2, P, 4], BF16, name=name, align_bytes=64)
+            nc.scalar.copy(out=grp[:].bitcast(F32), in_=bank[:].rearrange("p (s u) r -> p s r u", u=2))
+            return grp
+
+        def quantize(name, grp2d, width):
+            cod = sb.tile([P, width], U32, name=name + "_cod", align_bytes=64)
+            scl = sb.tile([P, width], U8, name=name + "_scl", align_bytes=64)
+            nc.vector.quantize_mx(out=cod[:].bitcast(FP8X4), scales=scl[:], in_=grp2d)
+            return cod, scl
+
+        def tx(g, b):
+            x_tp[g, b] = transpose_words("x_tp%d%d" % (g, b), x_raw[g, b][:].rearrange("p t k -> p (t k)"))
+
+        def cx(g, b):
+            x_grp[g, b] = group_words("x_grp%d%d" % (g, b), x_tp[g, b])
+
+        def qx(g, b):
+            x_cod[g, b], x_scl[g, b] = quantize("x%d%d" % (g, b), x_grp[g, b][:].rearrange("p s m j -> p (s m j)"), 256)
+
+        def wi(h):
+            w_grp[h] = sb.tile([P, P, 4], BF16, name="w_grp%d" % h, align_bytes=64)
+            nc.vector.tensor_copy(out=w_grp[h][:], in_=w_raw[h // 2][:, h % 2].rearrange("p j c -> p c j"))
+
+        def qw(h):
+            w_cod[h], w_scl[h] = quantize("w%d" % h, w_grp[h][:].rearrange("p c j -> p (c j)"), P)
+
+        def ta(i):
+            a_tp[i] = transpose_words("a_tp%d" % i, a_raw[i][:])
+
+        def ca(i):
+            a_grp[i] = group_words("a_grp%d" % i, a_tp[i])
+
+        def qa(i):
+            a_cod[i], a_scl[i] = quantize("a%d" % i, a_grp[i][:].rearrange("p g r j -> p (g r j)"), 256)
+
+        for g in range(2):
+            g_cod[g] = sb.tile([P, 512], U32, name="g_cod%d" % g, align_bytes=64)
+            g_scl[g] = sb.tile([P, 512], U8, name="g_scl%d" % g, align_bytes=64)
+
+        def s1(g, h):
+            g_ps[g, h] = ps.tile([P, 4, P], G_BANK_DT, name="g_ps%d%d" % (g, h), tag="acc", bufs=ACC_BANKS)
+            for t in range(4):
+                cols = slice(P * (t % 2), P * (t % 2 + 1))
+                nc.tensor.matmul_mx(out=g_ps[g, h][:, t, :],
+                                    lhsT=x_cod[g, t // 2][:, cols].bitcast(FP8X4), lhsT_scale=x_scl[g, t // 2][:, cols],
+                                    rhs=w_cod[h][:].bitcast(FP8X4), rhs_scale=w_scl[h][:],
+                                    start=True, stop=True)
+
+        def cg(g, h):
+            g_grp[g, h] = sb.tile([P, P, 4], BF16, name="g_grp%d%d" % (g, h), align_bytes=64)
+            if h < 3:
+                nc.scalar.copy(out=g_grp[g, h][:], in_=g_ps[g, h][:].rearrange("p t c -> p c t"))
+            else:
+                nc.vector.tensor_copy(out=g_grp[g, h][:], in_=g_ps[g, h][:].rearrange("p t c -> p c t"))
+
+        def qg(g, h):
+            cols = slice(P * h, P * (h + 1))
+            nc.vector.quantize_mx(out=g_cod[g][:, cols].bitcast(FP8X4), scales=g_scl[g][:, cols],
+                                  in_=g_grp[g, h][:].rearrange("p c t -> p (c t)"))
+
+        def s2(i):
+            p_ps[i] = ps.tile([P, 512], F32, name="p_ps%d" % i, tag="acc", bufs=ACC_BANKS)
+            for g in range(2):
+                cols = slice(P * g, P * (g + 1))
+                nc.tensor.matmul_mx(out=p_ps[i][:],
+                                    lhsT=a_cod[i][:, cols].bitcast(FP8X4), lhsT_scale=a_scl[i][:, cols],
+                                    rhs=g_cod[g][:].bitcast(FP8X4), rhs_scale=g_scl[g][:],
+                                    start=(g == 0), stop=(g == 1))
+
+        def ee(i):
+            e_sb[i] = sb.tile([P, 512], F32, name="e_sb%d" % i)
+            nc.scalar.activation(out=e_sb[i][:], in_=p_ps[i][:], func=ACTF.Exp)
+
+        def mm(i):
+            q_sb[i] = sb.tile([P, 512], F32, name="q_sb%d" % i)
+            if i < 6:
+                nc.vector.tensor_scalar(out=q_sb[i][:], in0=e_sb[i][:], scalar1=-1.0, scalar2=0.0,
+                                        op0=ALU.add, op1=ALU.min)
+            else:
+                nc.scalar.activation(out=q_sb[i][:], in_=e_sb[i][:], func=ACTF.Relu, scale=-1.0, bias=1.0)
+
+        def ff(i):
+            o_sb = sb.tile([P, 512], F32, name="o_sb%d" % i)
+            nc.vector.scalar_tensor_tensor(out=o_sb[:], in0=p_ps[i][:], scalar=0.0, in1=q_sb[i][:],
+                                           op0=ALU.max, op1=(ALU.add if i < 6 else ALU.subtract))
+            nc.sync.dma_start(out=out[P * i:P * (i + 1), :], in_=o_sb[:])
+
+        keep_clock(4)
+        tx(0, 0)
+        tx(0, 1)
+        keep_clock(2)
+        tx(1, 0)
+        cx(0, 0)
+        tx(1, 1)
+        cx(0, 1)
+        cx(1, 0)
+        cx(1, 1)
+        qx(0, 0)
+        wi(0)
+        qx(0, 1)
+        wi(1)
+        qw(0)
+        qw(1)
+        wi(2)
+        qx(1, 0)
+        wi(3)
+        qw(2)
+        qx(1, 1)
+        qw(3)
+
+        for g in range(2):
+            s1(g, 0)
+            s1(g, 1)
+            ta(g)
+            s1(g, 2)
+            s1(g, 3)
+            cg(g, 0)
+            cg(g, 1)
+            cg(g, 2)
+            ca(g)
+            qg(g, 0)
+            qg(g, 1)
+            cg(g, 3)
+            qg(g, 2)
+            qg(g, 3)
+            qa(g)
+
+        for j in range(4):
+            now = [2 * j, 2 * j + 1]
+            ahead = [2 * j + 2, 2 * j + 3] if j < 3 else []
+            for i in ahead:
+                ta(i)
+            for i in now:
+                s2(i)
+            for i in ahead:
+                ca(i)
+            for i in now:
+                ee(i)
+            for k in range(2):
+                if j > 0:
+                    ff(2 * j - 2 + k)
+                if j < 3:
+                    qa(2 * j + 2 + k)
+            for i in now:
+                mm(i)
+        ff(6)
+        ff(7)

@@ -76,9 +76,10 @@ def tile_gat_pa_kernel(tc, x, adj, W0, out):
                     nc.tensor.transpose(bank[:, 2 * s + u, :], words[:, 256 * s + u:256 * (s + 1):2], ident[:])
             return bank
 
-        def group_words(name, bank):
+        def group_words(name, bank, on_vector=False):
             grp = sb.tile([P, 2, P, 4], BF16, name=name, align_bytes=64)
-            nc.scalar.copy(out=grp[:].bitcast(F32), in_=bank[:].rearrange("p (s u) r -> p s r u", u=2))
+            copy = nc.vector.tensor_copy if on_vector else nc.scalar.copy
+            copy(out=grp[:].bitcast(F32), in_=bank[:].rearrange("p (s u) r -> p s r u", u=2))
             return grp
 
         def quantize(name, grp2d, width):
@@ -98,7 +99,8 @@ def tile_gat_pa_kernel(tc, x, adj, W0, out):
 
         def wi(h):
             w_grp[h] = sb.tile([P, P, 4], BF16, name="w_grp%d" % h, align_bytes=64)
-            nc.vector.tensor_copy(out=w_grp[h][:], in_=w_raw[h // 2][:, h % 2].rearrange("p j c -> p c j"))
+            copy = nc.scalar.copy if h == 1 else nc.vector.tensor_copy
+            copy(out=w_grp[h][:], in_=w_raw[h // 2][:, h % 2].rearrange("p j c -> p c j"))
 
         def qw(h):
             w_cod[h], w_scl[h] = quantize("w%d" % h, w_grp[h][:].rearrange("p c j -> p (c j)"), P)
@@ -107,7 +109,7 @@ def tile_gat_pa_kernel(tc, x, adj, W0, out):
             a_tp[i] = transpose_words("a_tp%d" % i, a_raw[i][:])
 
         def ca(i):
-            a_grp[i] = group_words("a_grp%d" % i, a_tp[i])
+            a_grp[i] = group_words("a_grp%d" % i, a_tp[i], on_vector=(i == 0))
 
         def qa(i):
             a_cod[i], a_scl[i] = quantize("a%d" % i, a_grp[i][:].rearrange("p g r j -> p (g r j)"), 256)
@@ -172,20 +174,20 @@ def tile_gat_pa_kernel(tc, x, adj, W0, out):
         cx(0, 0)
         tx(1, 1)
         cx(0, 1)
+        wi(1)
         cx(1, 0)
         cx(1, 1)
         qx(0, 0)
         wi(0)
         qx(0, 1)
-        wi(1)
         qw(0)
         qw(1)
         wi(2)
-        qx(1, 0)
         wi(3)
         qw(2)
-        qx(1, 1)
         qw(3)
+        qx(1, 0)
+        qx(1, 1)
 
         for g in range(2):
             s1(g, 0)
@@ -193,10 +195,13 @@ def tile_gat_pa_kernel(tc, x, adj, W0, out):
             ta(g)
             s1(g, 2)
             s1(g, 3)
+            if g == 0:
+                ca(0)
             cg(g, 0)
             cg(g, 1)
             cg(g, 2)
-            ca(g)
+            if g == 1:
+                ca(1)
             qg(g, 0)
             qg(g, 1)
             cg(g, 3)
@@ -215,11 +220,12 @@ def tile_gat_pa_kernel(tc, x, adj, W0, out):
                 ca(i)
             for i in now:
                 ee(i)
-            for k in range(2):
-                if j > 0:
-                    ff(2 * j - 2 + k)
-                if j < 3:
-                    qa(2 * j + 2 + k)
+            if j > 0:
+                ff(2 * j - 2)
+            for i in ahead:
+                qa(i)
+            if j > 0:
+                ff(2 * j - 1)
             for i in now:
                 mm(i)
         ff(6)

@@ -32,24 +32,27 @@ def tile_gat_pa_kernel(tc, x, adj, W0, out):
         g_ps, g_grp, g_cod, g_scl = {}, {}, {}, {}
         p_ps, e_sb, q_sb = {}, {}, {}
 
-        def load_x(g, b):
-            x_raw[g, b] = sb.tile([P, 2, 512], BF16, name="x_raw%d%d" % (g, b))
+        def load_x(g, t0, n):
+            raw = sb.tile([P, n, 512], BF16, name="x_raw%d%d" % (g, t0))
             rows = x[512 * g:512 * (g + 1), :].rearrange("(m t) k -> m t k", t=4)
-            nc.sync.dma_start(out=x_raw[g, b][:], in_=rows[:, 2 * b:2 * b + 2, :])
+            nc.sync.dma_start(out=raw[:], in_=rows[:, t0:t0 + n, :])
+            for s in range(n):
+                x_raw[g, t0 + s] = raw[:, s, :]
 
         def load_w(a):
             w_raw[a] = sb.tile([P, 2, 4, P], BF16, name="w_raw%d" % a)
             nc.sync.dma_start(out=w_raw[a][:], in_=W0[2 * a:2 * a + 2].rearrange("h (p j) c -> p h j c", j=4))
 
         def load_adj(i):
-            a_raw[i] = sb.tile([P, 1024], BF16, name="a_raw%d" % i)
-            nc.sync.dma_start(out=a_raw[i][:], in_=adj[P * i:P * (i + 1), :])
+            a_raw[i] = sb.tile([P, 2, 512], BF16, name="a_raw%d" % i)
+            nc.sync.dma_start(out=a_raw[i][:], in_=adj[P * i:P * (i + 1), :].rearrange("n (g m) -> n g m", g=2))
 
-        load_x(0, 0)
-        load_x(0, 1)
-        load_x(1, 0)
+        load_x(0, 0, 2)
+        load_x(0, 2, 2)
+        load_x(1, 0, 2)
         load_w(0)
-        load_x(1, 1)
+        load_x(1, 2, 1)
+        load_x(1, 3, 1)
         load_w(1)
         for i in range(8):
             load_adj(i)
@@ -68,12 +71,12 @@ def tile_gat_pa_kernel(tc, x, adj, W0, out):
             for r in range(n):
                 nc.tensor.matmul(out=idle_ps[:], lhsT=zeros[:, 0:P], rhs=zeros[:], start=True, stop=True)
 
-        def transpose_words(name, raw2d):
+        def transpose_words(name, rows512):
             bank = ps.tile([P, 4, P], F32, name=name, tag="tp", bufs=TP_BANKS)
-            words = raw2d.bitcast(F32)
             for s in range(2):
+                words = rows512[s].bitcast(F32)
                 for u in range(2):
-                    nc.tensor.transpose(bank[:, 2 * s + u, :], words[:, 256 * s + u:256 * (s + 1):2], ident[:])
+                    nc.tensor.transpose(bank[:, 2 * s + u, :], words[:, u:256:2], ident[:])
             return bank
 
         def group_words(name, bank, on_vector=False):
@@ -89,7 +92,7 @@ def tile_gat_pa_kernel(tc, x, adj, W0, out):
             return cod, scl
 
         def tx(g, b):
-            x_tp[g, b] = transpose_words("x_tp%d%d" % (g, b), x_raw[g, b][:].rearrange("p t k -> p (t k)"))
+            x_tp[g, b] = transpose_words("x_tp%d%d" % (g, b), [x_raw[g, 2 * b], x_raw[g, 2 * b + 1]])
 
         def cx(g, b):
             x_grp[g, b] = group_words("x_grp%d%d" % (g, b), x_tp[g, b])
@@ -106,7 +109,7 @@ def tile_gat_pa_kernel(tc, x, adj, W0, out):
             w_cod[h], w_scl[h] = quantize("w%d" % h, w_grp[h][:].rearrange("p c j -> p (c j)"), P)
 
         def ta(i):
-            a_tp[i] = transpose_words("a_tp%d" % i, a_raw[i][:])
+            a_tp[i] = transpose_words("a_tp%d" % i, [a_raw[i][:, 0, :], a_raw[i][:, 1, :]])
 
         def ca(i):
             a_grp[i] = group_words("a_grp%d" % i, a_tp[i], on_vector=(i == 0))
@@ -129,42 +132,43 @@ def tile_gat_pa_kernel(tc, x, adj, W0, out):
 
         def cg(g, h):
             g_grp[g, h] = sb.tile([P, P, 4], BF16, name="g_grp%d%d" % (g, h), align_bytes=64)
-            if h < 3:
-                nc.scalar.copy(out=g_grp[g, h][:], in_=g_ps[g, h][:].rearrange("p t c -> p c t"))
-            else:
-                nc.vector.tensor_copy(out=g_grp[g, h][:], in_=g_ps[g, h][:].rearrange("p t c -> p c t"))
+            copy = nc.scalar.copy if h < 3 else nc.vector.tensor_copy
+            copy(out=g_grp[g, h][:], in_=g_ps[g, h][:].rearrange("p t c -> p c t"))
 
         def qg(g, h):
             cols = slice(P * h, P * (h + 1))
             nc.vector.quantize_mx(out=g_cod[g][:, cols].bitcast(FP8X4), scales=g_scl[g][:, cols],
                                   in_=g_grp[g, h][:].rearrange("p c t -> p (c t)"))
 
-        def s2(i):
-            p_ps[i] = ps.tile([P, 512], F32, name="p_ps%d" % i, tag="acc", bufs=ACC_BANKS)
+        def s2(piece):
+            i, c0, width = piece
+            p_ps[piece] = ps.tile([P, width], F32, name="p_ps%d_%d" % (i, c0), tag="acc", bufs=ACC_BANKS)
             for g in range(2):
-                cols = slice(P * g, P * (g + 1))
-                nc.tensor.matmul_mx(out=p_ps[i][:],
-                                    lhsT=a_cod[i][:, cols].bitcast(FP8X4), lhsT_scale=a_scl[i][:, cols],
-                                    rhs=g_cod[g][:].bitcast(FP8X4), rhs_scale=g_scl[g][:],
+                rows = slice(P * g, P * (g + 1))
+                cols = slice(c0, c0 + width)
+                nc.tensor.matmul_mx(out=p_ps[piece][:],
+                                    lhsT=a_cod[i][:, rows].bitcast(FP8X4), lhsT_scale=a_scl[i][:, rows],
+                                    rhs=g_cod[g][:, cols].bitcast(FP8X4), rhs_scale=g_scl[g][:, cols],
                                     start=(g == 0), stop=(g == 1))
 
-        def ee(i):
-            e_sb[i] = sb.tile([P, 512], F32, name="e_sb%d" % i)
-            nc.scalar.activation(out=e_sb[i][:], in_=p_ps[i][:], func=ACTF.Exp)
+        def ee(piece):
+            e_sb[piece] = sb.tile([P, piece[2]], F32, name="e_sb%d_%d" % piece[0:2])
+            nc.scalar.activation(out=e_sb[piece][:], in_=p_ps[piece][:], func=ACTF.Exp)
 
-        def mm(i):
-            q_sb[i] = sb.tile([P, 512], F32, name="q_sb%d" % i)
-            if i < 6:
-                nc.vector.tensor_scalar(out=q_sb[i][:], in0=e_sb[i][:], scalar1=-1.0, scalar2=0.0,
-                                        op0=ALU.add, op1=ALU.min)
+        def mm(piece):
+            q_sb[piece] = sb.tile([P, piece[2]], F32, name="q_sb%d_%d" % piece[0:2])
+            if piece[0] == 6:
+                nc.scalar.activation(out=q_sb[piece][:], in_=e_sb[piece][:], func=ACTF.Relu, scale=-1.0, bias=1.0)
             else:
-                nc.scalar.activation(out=q_sb[i][:], in_=e_sb[i][:], func=ACTF.Relu, scale=-1.0, bias=1.0)
+                nc.vector.tensor_scalar(out=q_sb[piece][:], in0=e_sb[piece][:], scalar1=-1.0, scalar2=0.0,
+                                        op0=ALU.add, op1=ALU.min)
 
-        def ff(i):
-            o_sb = sb.tile([P, 512], F32, name="o_sb%d" % i)
-            nc.vector.scalar_tensor_tensor(out=o_sb[:], in0=p_ps[i][:], scalar=0.0, in1=q_sb[i][:],
-                                           op0=ALU.max, op1=(ALU.add if i < 6 else ALU.subtract))
-            nc.sync.dma_start(out=out[P * i:P * (i + 1), :], in_=o_sb[:])
+        def ff(piece):
+            i, c0, width = piece
+            o_sb = sb.tile([P, width], F32, name="o_sb%d_%d" % (i, c0))
+            nc.vector.scalar_tensor_tensor(out=o_sb[:], in0=p_ps[piece][:], scalar=0.0, in1=q_sb[piece][:],
+                                           op0=ALU.max, op1=(ALU.subtract if i == 6 else ALU.add))
+            nc.sync.dma_start(out=out[P * i:P * (i + 1), c0:c0 + width], in_=o_sb[:])
 
         keep_clock(4)
         tx(0, 0)
@@ -209,24 +213,36 @@ def tile_gat_pa_kernel(tc, x, adj, W0, out):
             qg(g, 3)
             qa(g)
 
-        for j in range(4):
-            now = [2 * j, 2 * j + 1]
-            ahead = [2 * j + 2, 2 * j + 3] if j < 3 else []
+        whole = [(i, 0, 512) for i in range(7)]
+        halves = [(7, 0, 256), (7, 256, 256)]
+        for j in range(3):
+            now = whole[2 * j:2 * j + 2]
+            ahead = [2 * j + 2, 2 * j + 3]
             for i in ahead:
                 ta(i)
-            for i in now:
-                s2(i)
+            for piece in now:
+                s2(piece)
             for i in ahead:
                 ca(i)
-            for i in now:
-                ee(i)
+            for piece in now:
+                ee(piece)
             if j > 0:
-                ff(2 * j - 2)
+                ff(whole[2 * j - 2])
             for i in ahead:
                 qa(i)
             if j > 0:
-                ff(2 * j - 1)
-            for i in now:
-                mm(i)
-        ff(6)
-        ff(7)
+                ff(whole[2 * j - 1])
+            for piece in now:
+                mm(piece)
+        for piece in [whole[6]] + halves:
+            s2(piece)
+        ee(whole[6])
+        mm(whole[6])
+        for piece in halves:
+            ee(piece)
+        for piece in whole[4:7]:
+            ff(piece)
+        for piece in halves:
+            mm(piece)
+        for piece in halves:
+            ff(piece)

from contextlib import ExitStack

import concourse.mybir as mybir
from concourse.masks import make_identity

FLOPS = 2 * 1024 * 512 * 512 + 2 * 1024 * 1024 * 512

F32 = mybir.dt.float32
BF16 = mybir.dt.bfloat16
U32 = mybir.dt.uint32
U8 = mybir.dt.uint8
FP8X4 = mybir.dt.float8_e4m3fn_x4
ALU = mybir.AluOpType
ACTF = mybir.ActivationFunctionType

P = 128
G_BANK_DT = F32
TP_BANKS = 3
ACC_BANKS = 5


def tile_gat_pa_kernel(tc, x, adj, W0, out):
    nc = tc.nc
    with ExitStack() as ctx:
        sb = ctx.enter_context(tc.tile_pool(name="sb", bufs=1))
        ps = ctx.enter_context(tc.psum_pool(name="ps", bufs=1))
        ctx.enter_context(tc.manual_schedule())

        x_raw, x_tp, x_grp, x_cod, x_scl = {}, {}, {}, {}, {}
        w_raw, w_grp, w_cod, w_scl = {}, {}, {}, {}
        a_raw, a_tp, a_grp, a_cod, a_scl = {}, {}, {}, {}, {}
        g_ps, g_grp, g_cod, g_scl = {}, {}, {}, {}
        p_ps, e_sb, q_sb = {}, {}, {}

        def load_x(g, t0, n):
            raw = sb.tile([P, n, 512], BF16, name="x_raw%d%d" % (g, t0))
            rows = x[512 * g:512 * (g + 1), :].rearrange("(m t) k -> m t k", t=4)
            nc.sync.dma_start(out=raw[:], in_=rows[:, t0:t0 + n, :])
            for s in range(n):
                x_raw[g, t0 + s] = raw[:, s, :]

        def load_w(a):
            w_raw[a] = sb.tile([P, 2, 4, P], BF16, name="w_raw%d" % a)
            nc.sync.dma_start(out=w_raw[a][:], in_=W0[2 * a:2 * a + 2].rearrange("h (p j) c -> p h j c", j=4))

        def load_adj(i):
            a_raw[i] = sb.tile([P, 2, 512], BF16, name="a_raw%d" % i)
            nc.sync.dma_start(out=a_raw[i][:], in_=adj[P * i:P * (i + 1), :].rearrange("n (g m) -> n g m", g=2))

        load_x(0, 0, 2)
        load_x(0, 2, 2)
        load_x(1, 0, 2)
        load_w(0)
        load_x(1, 2, 1)
        load_x(1, 3, 1)
        load_w(1)
        for i in range(8):
            load_adj(i)

        zeros = sb.tile([P, 512], BF16, name="zeros")
        nc.vector.memset(zeros[:], 0.0)
        idle_ps = ps.tile([P, 512], F32, name="idle_ps", tag="acc", bufs=ACC_BANKS)
        exp_in = sb.tile([P, 1], F32, name="exp_in")
        exp_out = sb.tile([P, 1], F32, name="exp_out")
        nc.vector.memset(exp_in[:], 0.0)
        nc.scalar.activation(out=exp_out[:], in_=exp_in[:], func=ACTF.Exp)
        ident = sb.tile([P, P], F32, name="ident")
        make_identity(nc, ident[:])

        def keep_clock(n):
            for r in range(n):
                nc.tensor.matmul(out=idle_ps[:], lhsT=zeros[:, 0:P], rhs=zeros[:], start=True, stop=True)

        def transpose_words(name, rows512):
            bank = ps.tile([P, 4, P], F32, name=name, tag="tp", bufs=TP_BANKS)
            for s in range(2):
                words = rows512[s].bitcast(F32)
                for u in range(2):
                    nc.tensor.transpose(bank[:, 2 * s + u, :], words[:, u:256:2], ident[:])
            return bank

        def group_words(name, bank, on_vector=False):
            grp = sb.tile([P, 2, P, 4], BF16, name=name, align_bytes=64)
            copy = nc.vector.tensor_copy if on_vector else nc.scalar.copy
            copy(out=grp[:].bitcast(F32), in_=bank[:].rearrange("p (s u) r -> p s r u", u=2))
            return grp

        def quantize(name, grp2d, width):
            cod = sb.tile([P, width], U32, name=name + "_cod", align_bytes=64)
            scl = sb.tile([P, width], U8, name=name + "_scl", align_bytes=64)
            nc.vector.quantize_mx(out=cod[:].bitcast(FP8X4), scales=scl[:], in_=grp2d)
            return cod, scl

        def tx(g, b):
            x_tp[g, b] = transpose_words("x_tp%d%d" % (g, b), [x_raw[g, 2 * b], x_raw[g, 2 * b + 1]])

        def cx(g, b):
            x_grp[g, b] = group_words("x_grp%d%d" % (g, b), x_tp[g, b])

        def qx(g, b):
            x_cod[g, b], x_scl[g, b] = quantize("x%d%d" % (g, b), x_grp[g, b][:].rearrange("p s m j -> p (s m j)"), 256)

        def wi(h):
            w_grp[h] = sb.tile([P, P, 4], BF16, name="w_grp%d" % h, align_bytes=64)
            copy = nc.scalar.copy if h == 1 else nc.vector.tensor_copy
            copy(out=w_grp[h][:], in_=w_raw[h // 2][:, h % 2].rearrange("p j c -> p c j"))

        def qw(h):
            w_cod[h], w_scl[h] = quantize("w%d" % h, w_grp[h][:].rearrange("p c j -> p (c j)"), P)

        def ta(i):
            a_tp[i] = transpose_words("a_tp%d" % i, [a_raw[i][:, 0, :], a_raw[i][:, 1, :]])

        def ca(i):
            a_grp[i] = group_words("a_grp%d" % i, a_tp[i], on_vector=(i == 0))

        def qa(i):
            a_cod[i], a_scl[i] = quantize("a%d" % i, a_grp[i][:].rearrange("p g r j -> p (g r j)"), 256)

        for g in range(2):
            g_cod[g] = sb.tile([P, 512], U32, name="g_cod%d" % g, align_bytes=64)
            g_scl[g] = sb.tile([P, 512], U8, name="g_scl%d" % g, align_bytes=64)

        def s1(g, h):
            g_ps[g, h] = ps.tile([P, 4, P], G_BANK_DT, name="g_ps%d%d" % (g, h), tag="acc", bufs=ACC_BANKS)
            for t in range(4):
                cols = slice(P * (t % 2), P * (t % 2 + 1))
                nc.tensor.matmul_mx(out=g_ps[g, h][:, t, :],
                                    lhsT=x_cod[g, t // 2][:, cols].bitcast(FP8X4), lhsT_scale=x_scl[g, t // 2][:, cols],
                                    rhs=w_cod[h][:].bitcast(FP8X4), rhs_scale=w_scl[h][:],
                                    start=True, stop=True)

        def cg(g, h):
            g_grp[g, h] = sb.tile([P, P, 4], BF16, name="g_grp%d%d" % (g, h), align_bytes=64)
            copy = nc.scalar.copy if h < 3 else nc.vector.tensor_copy
            copy(out=g_grp[g, h][:], in_=g_ps[g, h][:].rearrange("p t c -> p c t"))

        def qg(g, h):
            cols = slice(P * h, P * (h + 1))
            nc.vector.quantize_mx(out=g_cod[g][:, cols].bitcast(FP8X4), scales=g_scl[g][:, cols],
                                  in_=g_grp[g, h][:].rearrange("p c t -> p (c t)"))

        def s2(piece):
            i, c0, width = piece
            p_ps[piece] = ps.tile([P, width], F32, name="p_ps%d_%d" % (i, c0), tag="acc", bufs=ACC_BANKS)
            for g in range(2):
                rows = slice(P * g, P * (g + 1))
                cols = slice(c0, c0 + width)
                nc.tensor.matmul_mx(out=p_ps[piece][:],
                                    lhsT=a_cod[i][:, rows].bitcast(FP8X4), lhsT_scale=a_scl[i][:, rows],
                                    rhs=g_cod[g][:, cols].bitcast(FP8X4), rhs_scale=g_scl[g][:, cols],
                                    start=(g == 0), stop=(g == 1))

        def ee(piece):
            e_sb[piece] = sb.tile([P, piece[2]], F32, name="e_sb%d_%d" % piece[0:2])
            nc.scalar.activation(out=e_sb[piece][:], in_=p_ps[piece][:], func=ACTF.Exp)

        def mm(piece):
            q_sb[piece] = sb.tile([P, piece[2]], F32, name="q_sb%d_%d" % piece[0:2])
            if piece[0] == 6:
                nc.scalar.activation(out=q_sb[piece][:], in_=e_sb[piece][:], func=ACTF.Relu, scale=-1.0, bias=1.0)
            else:
                nc.vector.tensor_scalar(out=q_sb[piece][:], in0=e_sb[piece][:], scalar1=-1.0, scalar2=0.0,
                                        op0=ALU.add, op1=ALU.min)

        def ff(piece):
            i, c0, width = piece
            o_sb = sb.tile([P, width], F32, name="o_sb%d_%d" % (i, c0))
            nc.vector.scalar_tensor_tensor(out=o_sb[:], in0=p_ps[piece][:], scalar=0.0, in1=q_sb[piece][:],
                                           op0=ALU.max, op1=(ALU.subtract if i == 6 else ALU.add))
            nc.sync.dma_start(out=out[P * i:P * (i + 1), c0:c0 + width], in_=o_sb[:])

        keep_clock(4)
        tx(0, 0)
        tx(0, 1)
        keep_clock(2)
        tx(1, 0)
        cx(0, 0)
        tx(1, 1)
        cx(0, 1)
        wi(1)
        cx(1, 0)
        cx(1, 1)
        qx(0, 0)
        wi(0)
        qx(0, 1)
        qw(0)
        qw(1)
        wi(2)
        wi(3)
        qw(2)
        qw(3)
        qx(1, 0)
        qx(1, 1)

        for g in range(2):
            s1(g, 0)
            s1(g, 1)
            ta(g)
            s1(g, 2)
            s1(g, 3)
            if g == 0:
                ca(0)
            cg(g, 0)
            cg(g, 1)
            cg(g, 2)
            if g == 1:
                ca(1)
            qg(g, 0)
            qg(g, 1)
            cg(g, 3)
            qg(g, 2)
            qg(g, 3)
            qa(g)

        whole = [(i, 0, 512) for i in range(7)]
        halves = [(7, 0, 256), (7, 256, 256)]
        for j in range(3):
            now = whole[2 * j:2 * j + 2]
            ahead = [2 * j + 2, 2 * j + 3]
            for i in ahead:
                ta(i)
            for piece in now:
                s2(piece)
            for i in ahead:
                ca(i)
            for piece in now:
                ee(piece)
            if j > 0:
                ff(whole[2 * j - 2])
            for i in ahead:
                qa(i)
            if j > 0:
                ff(whole[2 * j - 1])
            for piece in now:
                mm(piece)
        for piece in [whole[6]] + halves:
            s2(piece)
        ee(whole[6])
        mm(whole[6])
        for piece in halves:
            ee(piece)
        for piece in whole[4:7]:
            ff(piece)
        for piece in halves:
            mm(piece)
        for piece in halves:
            ff(piece)
